import numpy as np
import ml_dtypes


def mxq(x, axis, fmt="e4m3"):
    dtype, down = {"e4m3": (ml_dtypes.float8_e4m3fn, 7), "e5m2": (ml_dtypes.float8_e5m2, 14)}[fmt]
    v = np.moveaxis(np.asarray(x, np.float32).astype(ml_dtypes.bfloat16).astype(np.float64), axis, -1)
    blocks = v.reshape(v.shape[:-1] + (-1, 32))
    amax = np.abs(blocks).max(-1, keepdims=True)
    byte = np.maximum(np.where(amax > 0, np.frexp(amax)[1] - 1 + 127, 0) - down, 1)
    scale = np.exp2(byte - 127.0)
    codes = (blocks / scale).astype(np.float32).astype(dtype).astype(np.float64)
    return np.moveaxis((codes * scale).reshape(v.shape), -1, axis)


WIDE = False


def mx_kscale(k):
    if not WIDE:
        return np.ones(k)
    levels = np.array([10, -10, 5, -5, 0])
    a = np.random.permutation(np.resize(levels, k // 512 * 4)).reshape(k // 512, 4)
    idx = np.arange(k)
    return np.exp2(a[idx // 512, idx % 128 // 32])


BF16 = ml_dtypes.bfloat16


def bf(x):
    return np.asarray(x, np.float32).astype(BF16)


def f64(x):
    return np.asarray(x).astype(np.float64)


B, S, D, QK, EXP = 16, 512, 1024, 32, 32
EPS = 1e-5
W = QK + QK + EXP + EXP
NT = 110


def erf(v):
    a = np.minimum(np.abs(v), 6.0)
    c = 2.0 * a * a
    term = a.copy()
    total = a.copy()
    for n in range(1, NT):
        term = term * c / (2.0 * n + 1.0)
        total = total + term
    return np.sign(v) * (2.0 / np.sqrt(np.pi)) * np.exp(-a * a) * total


def gelu(v):
    return 0.5 * v * (1.0 + erf(v / np.sqrt(2.0)))


def setup_inputs():
    s = mx_kscale(D)
    row_gain = np.exp(0.5 * np.random.standard_normal((B, S)))[..., None]
    row_shift = 0.5 * np.random.standard_normal((B, S))[..., None]
    return {"x": bf(np.random.standard_normal((B, S, D)) * row_gain + row_shift),
            "ln_gamma": bf((1.0 + 0.1 * np.random.standard_normal(D)) * s),
            "ln_beta": bf(0.1 * np.random.standard_normal(D) * s),
            "expand": bf(np.random.standard_normal((W, D)) / np.sqrt(D) / s[None, :])}


def reference(x, ln_gamma, ln_beta, expand):
    x = f64(x)
    mu = x.mean(-1, keepdims=True)
    var = x.var(-1, keepdims=True)
    h = (x - mu) / np.sqrt(var + EPS) * f64(ln_gamma) + f64(ln_beta)
    fused = mxq(h, 2, "e4m3") @ mxq(f64(expand), 1, "e4m3").T
    query = fused[..., :QK]
    key = fused[..., QK:QK + QK]
    linear = fused[..., QK + QK:QK + QK + EXP]
    pre_gelu = fused[..., QK + QK + EXP:]
    geglu = linear * gelu(pre_gelu)
    return query, key, geglu

@@ -1,0 +1,167 @@
+from contextlib import ExitStack
+
+import concourse.mybir as mybir
+from concourse.masks import make_identity
+
+F32 = mybir.dt.float32
+BF16 = mybir.dt.bfloat16
+U32 = mybir.dt.uint32
+U8 = mybir.dt.uint8
+I32 = mybir.dt.int32
+FP8X4 = mybir.dt.float8_e4m3fn_x4
+ALU = mybir.AluOpType
+ACT = mybir.ActivationFunctionType
+
+P = 128
+ROWS = 16 * 512
+D = 1024
+W = 128
+QK = 32
+EPS = 1e-5
+PACK = 4
+K_PASS = P * PACK
+PASSES = D // K_PASS
+CHUNKS = D // P
+BN_MAX = 512
+TILES = 4
+GROUP_COLS = TILES * P
+ROWS_PER_PARTITION = ROWS // P
+GROUPS = ROWS_PER_PARTITION // TILES
+
+FLOPS = 2 * ROWS * D * W
+
+
+def tile_latentattentionblock_pa_t_kernel(tc, x, ln_gamma, ln_beta, expand, out_0, out_1, out_2):
+    nc = tc.nc
+    x_rows = x.flatten_outer_dims().rearrange("(p j) d -> p j d", p=P)
+    out_rows = [o.flatten_outer_dims().rearrange("(p j) c -> p j c", p=P) for o in (out_0, out_1, out_2)]
+
+    with ExitStack() as stack:
+        const = stack.enter_context(tc.tile_pool(name="const", bufs=1))
+
+        ident_f32 = const.tile([P, P], F32)
+        make_identity(nc, ident_f32[:])
+        ident_bf16 = const.tile([P, P], BF16)
+        make_identity(nc, ident_bf16[:])
+        minus_half = const.tile([P, TILES], F32)
+        nc.gpsimd.memset(minus_half[:], -0.5)
+
+        vec_rows = const.tile([P, P], BF16)
+        nc.vector.memset(vec_rows[:].bitcast(I32), 0)
+        nc.scalar.dma_start(out=vec_rows[0:CHUNKS, :], in_=ln_gamma.rearrange("(c p) -> c p", p=P))
+        nc.scalar.dma_start(out=vec_rows[CHUNKS : 2 * CHUNKS, :], in_=ln_beta.rearrange("(c p) -> c p", p=P))
+        expand_sb = const.tile([W, D], BF16)
+        nc.scalar.dma_start(out=expand_sb[:], in_=expand)
+
+        gain_shift = const.tile([P, 2 * CHUNKS], F32)
+        e_grouped = const.tile([P, PASSES, W, PACK], BF16, align_bytes=64)
+        e_codes = const.tile([P, PASSES, W], U32, align_bytes=64)
+        e_scales = const.tile([P, PASSES, W], U8, align_bytes=64)
+        with tc.psum_pool(name="setup_psum", bufs=1) as setup_psum:
+            vec_cols = setup_psum.tile([P, P], BF16)
+            nc.tensor.transpose(vec_cols[:], vec_rows[:], ident_bf16[:])
+            nc.vector.tensor_copy(out=gain_shift[:], in_=vec_cols[:, 0 : 2 * CHUNKS])
+            for g in range(PASSES):
+                e_t = setup_psum.tile([P, PACK, W], BF16, name="e_t%d" % g)
+                for t in range(PACK):
+                    c = PACK * g + t
+                    nc.tensor.transpose(e_t[:, t, :], expand_sb[:, c * P : (c + 1) * P], ident_bf16[:])
+                nc.vector.tensor_copy(out=e_grouped[:, g, :, :], in_=e_t[:].rearrange("p t o -> p o t"))
+            nc.vector.quantize_mx(
+                out=e_codes[:].rearrange("p g o -> p (g o)").bitcast(FP8X4),
+                scales=e_scales[:].rearrange("p g o -> p (g o)"),
+                in_=e_grouped[:].rearrange("p g o t -> p (g o t)"),
+            )
+
+        x_pool = stack.enter_context(tc.tile_pool(name="x_pool", bufs=4))
+        small = stack.enter_context(tc.tile_pool(name="small", bufs=4))
+        work = stack.enter_context(tc.tile_pool(name="work", bufs=2))
+        out_pool = stack.enter_context(tc.tile_pool(name="out_pool", bufs=3))
+        xt_psum = stack.enter_context(tc.psum_pool(name="xt_psum", bufs=6))
+        acc_psum = stack.enter_context(tc.psum_pool(name="acc_psum", bufs=2))
+
+        for i in range(GROUPS):
+            group_rows = slice(i * TILES, (i + 1) * TILES)
+            x_sb = x_pool.tile([P, TILES, D], BF16)
+            nc.sync.dma_start(out=x_sb[:], in_=x_rows[:, group_rows, :])
+
+            stats = small.tile([P, TILES, D // BN_MAX, 6], F32)
+            mean_var = small.tile([P, TILES, 2], F32)
+            for j in range(TILES):
+                for b in range(D // BN_MAX):
+                    nc.vector.bn_stats(out=stats[:, j, b, :], in_=x_sb[:, j, b * BN_MAX : (b + 1) * BN_MAX])
+                nc.vector.bn_aggr(out=mean_var[:, j, :], in_=stats[:, j, :, :].rearrange("p b s -> p (b s)"))
+            minus_mean = small.tile([P, TILES], F32)
+            nc.gpsimd.tensor_scalar(
+                out=minus_mean[:], in0=mean_var[:, :, 0], scalar1=-1.0, scalar2=0.0, op0=ALU.mult, op1=ALU.add
+            )
+            var_eps = small.tile([P, TILES], F32)
+            nc.gpsimd.tensor_scalar(
+                out=var_eps[:], in0=mean_var[:, :, 1], scalar1=EPS, scalar2=1.0, op0=ALU.add, op1=ALU.mult
+            )
+            rstd = small.tile([P, TILES], F32)
+            nc.gpsimd.tensor_tensor(out=rstd[:], in0=var_eps[:], in1=minus_half[:], op=ALU.pow)
+
+            normed = work.tile([P, TILES, D], F32)
+            for j in range(TILES):
+                nc.gpsimd.tensor_scalar(
+                    out=normed[:, j, :],
+                    in0=x_sb[:, j, :],
+                    scalar1=minus_mean[:, j : j + 1],
+                    scalar2=rstd[:, j : j + 1],
+                    op0=ALU.add,
+                    op1=ALU.mult,
+                )
+
+            h_planes = work.tile([P, CHUNKS, GROUP_COLS], BF16)
+            for c in range(CHUNKS):
+                normed_t = xt_psum.tile([P, TILES, P], F32)
+                for j in range(TILES):
+                    nc.tensor.transpose(normed_t[:, j, :], normed[:, j, c * P : (c + 1) * P], ident_f32[:])
+                nc.scalar.activation(
+                    out=h_planes[:, c, :],
+                    in_=normed_t[:].rearrange("p j r -> p (j r)"),
+                    func=ACT.Identity,
+                    scale=gain_shift[:, c : c + 1],
+                    bias=gain_shift[:, CHUNKS + c : CHUNKS + c + 1],
+                )
+
+            h_grouped = work.tile([P, PASSES, GROUP_COLS, PACK], BF16, align_bytes=64)
+            h_codes = work.tile([P, PASSES, GROUP_COLS], U32, align_bytes=64)
+            h_scales = work.tile([P, PASSES, GROUP_COLS], U8, align_bytes=64)
+            for g in range(PASSES):
+                nc.vector.tensor_copy(
+                    out=h_grouped[:, g, :, :].rearrange("p (q s) t -> p q t s", s=4),
+                    in_=h_planes[:, g * PACK : (g + 1) * PACK, :].rearrange("p t (q s) -> p q t s", s=4),
+                )
+            for g in range(PASSES):
+                nc.vector.quantize_mx(
+                    out=h_codes[:, g, :].bitcast(FP8X4),
+                    scales=h_scales[:, g, :],
+                    in_=h_grouped[:, g, :, :].rearrange("p r t -> p (r t)"),
+                )
+
+            fused = acc_psum.tile([P, TILES, W], F32)
+            for j in range(TILES):
+                tile_cols = slice(j * P, (j + 1) * P)
+                for g in range(PASSES):
+                    nc.tensor.matmul_mx(
+                        out=fused[:, j, :],
+                        lhsT=h_codes[:, g, tile_cols].bitcast(FP8X4),
+                        lhsT_scale=h_scales[:, g, tile_cols],
+                        rhs=e_codes[:, g, :].bitcast(FP8X4),
+                        rhs_scale=e_scales[:, g, :],
+                        start=(g == 0),
+                        stop=(g == PASSES - 1),
+                    )
+
+            results = out_pool.tile([P, 3, TILES, QK], F32)
+            nc.scalar.copy(
+                out=results[:, 0:2, :, :],
+                in_=fused[:, :, 0 : 2 * QK].rearrange("p j (w c) -> p w j c", w=2),
+            )
+            gelu = out_pool.tile([P, TILES, QK], F32)
+            nc.scalar.activation(out=gelu[:], in_=fused[:, :, 3 * QK : 4 * QK], func=ACT.Gelu)
+            nc.vector.tensor_tensor(out=results[:, 2, :, :], in0=fused[:, :, 2 * QK : 3 * QK], in1=gelu[:], op=ALU.mult)
+            for w in range(3):
+                nc.sync.dma_start(out=out_rows[w][:, group_rows, :], in_=results[:, w, :, :])

@@ -27,6 +27,8 @@ TILES = 4
 GROUP_COLS = TILES * P
 ROWS_PER_PARTITION = ROWS // P
 GROUPS = ROWS_PER_PARTITION // TILES
+X_BUFS = 4
+STAGE_BUFS = 3
 
 FLOPS = 2 * ROWS * D * W
 
@@ -73,36 +75,41 @@ def tile_latentattentionblock_pa_t_kernel(tc, x, ln_gamma, ln_beta, expand, out_
                 in_=e_grouped[:].rearrange("p g o t -> p (g o t)"),
             )
 
-        x_pool = stack.enter_context(tc.tile_pool(name="x_pool", bufs=4))
-        small = stack.enter_context(tc.tile_pool(name="small", bufs=4))
-        work = stack.enter_context(tc.tile_pool(name="work", bufs=2))
-        out_pool = stack.enter_context(tc.tile_pool(name="out_pool", bufs=3))
+        x_pool = stack.enter_context(tc.tile_pool(name="x_pool", bufs=X_BUFS))
+        small = stack.enter_context(tc.tile_pool(name="small", bufs=STAGE_BUFS))
+        work = stack.enter_context(tc.tile_pool(name="work", bufs=STAGE_BUFS))
+        out_pool = stack.enter_context(tc.tile_pool(name="out_pool", bufs=STAGE_BUFS))
         xt_psum = stack.enter_context(tc.psum_pool(name="xt_psum", bufs=6))
         acc_psum = stack.enter_context(tc.psum_pool(name="acc_psum", bufs=2))
 
-        for i in range(GROUPS):
-            group_rows = slice(i * TILES, (i + 1) * TILES)
-            x_sb = x_pool.tile([P, TILES, D], BF16)
-            nc.sync.dma_start(out=x_sb[:], in_=x_rows[:, group_rows, :])
+        live = {}
 
-            stats = small.tile([P, TILES, D // BN_MAX, 6], F32)
-            mean_var = small.tile([P, TILES, 2], F32)
+        def load(i):
+            x_sb = x_pool.tile([P, TILES, D], BF16, name="x_sb")
+            nc.sync.dma_start(out=x_sb[:], in_=x_rows[:, i * TILES : (i + 1) * TILES, :])
+            live["x", i] = x_sb
+
+        def statistics(i):
+            x_sb = live["x", i]
+            stats = small.tile([P, TILES, D // BN_MAX, 6], F32, name="stats")
+            mean_var = small.tile([P, TILES, 2], F32, name="mean_var")
             for j in range(TILES):
                 for b in range(D // BN_MAX):
                     nc.vector.bn_stats(out=stats[:, j, b, :], in_=x_sb[:, j, b * BN_MAX : (b + 1) * BN_MAX])
                 nc.vector.bn_aggr(out=mean_var[:, j, :], in_=stats[:, j, :, :].rearrange("p b s -> p (b s)"))
-            minus_mean = small.tile([P, TILES], F32)
-            nc.gpsimd.tensor_scalar(
-                out=minus_mean[:], in0=mean_var[:, :, 0], scalar1=-1.0, scalar2=0.0, op0=ALU.mult, op1=ALU.add
-            )
-            var_eps = small.tile([P, TILES], F32)
-            nc.gpsimd.tensor_scalar(
-                out=var_eps[:], in0=mean_var[:, :, 1], scalar1=EPS, scalar2=1.0, op0=ALU.add, op1=ALU.mult
-            )
-            rstd = small.tile([P, TILES], F32)
-            nc.gpsimd.tensor_tensor(out=rstd[:], in0=var_eps[:], in1=minus_half[:], op=ALU.pow)
+            minus_mean = small.tile([P, TILES], F32, name="minus_mean")
+            nc.vector.tensor_scalar_mul(out=minus_mean[:], in0=mean_var[:, :, 0], scalar1=-1.0)
+            var_eps = small.tile([P, TILES], F32, name="var_eps")
+            nc.vector.tensor_scalar_add(out=var_eps[:], in0=mean_var[:, :, 1], scalar1=EPS)
+            live["minus_mean", i] = minus_mean
+            live["var_eps", i] = var_eps
 
-            normed = work.tile([P, TILES, D], F32)
+        def normalise(i):
+            x_sb = live["x", i]
+            minus_mean = live["minus_mean", i]
+            rstd = small.tile([P, TILES], F32, name="rstd")
+            nc.gpsimd.tensor_tensor(out=rstd[:], in0=live["var_eps", i][:], in1=minus_half[:], op=ALU.pow)
+            normed = work.tile([P, TILES, D], F32, name="normed")
             for j in range(TILES):
                 nc.gpsimd.tensor_scalar(
                     out=normed[:, j, :],
@@ -112,10 +119,13 @@ def tile_latentattentionblock_pa_t_kernel(tc, x, ln_gamma, ln_beta, expand, out_
                     op0=ALU.add,
                     op1=ALU.mult,
                 )
+            live["normed", i] = normed
 
-            h_planes = work.tile([P, CHUNKS, GROUP_COLS], BF16)
+        def transpose_gain_shift(i):
+            normed = live["normed", i]
+            h_planes = work.tile([P, CHUNKS, GROUP_COLS], BF16, name="h_planes")
             for c in range(CHUNKS):
-                normed_t = xt_psum.tile([P, TILES, P], F32)
+                normed_t = xt_psum.tile([P, TILES, P], F32, name="normed_t")
                 for j in range(TILES):
                     nc.tensor.transpose(normed_t[:, j, :], normed[:, j, c * P : (c + 1) * P], ident_f32[:])
                 nc.scalar.activation(
@@ -125,23 +135,38 @@ def tile_latentattentionblock_pa_t_kernel(tc, x, ln_gamma, ln_beta, expand, out_
                     scale=gain_shift[:, c : c + 1],
                     bias=gain_shift[:, CHUNKS + c : CHUNKS + c + 1],
                 )
+            live["h_planes", i] = h_planes
 
-            h_grouped = work.tile([P, PASSES, GROUP_COLS, PACK], BF16, align_bytes=64)
-            h_codes = work.tile([P, PASSES, GROUP_COLS], U32, align_bytes=64)
-            h_scales = work.tile([P, PASSES, GROUP_COLS], U8, align_bytes=64)
-            for g in range(PASSES):
-                nc.vector.tensor_copy(
-                    out=h_grouped[:, g, :, :].rearrange("p (q s) t -> p q t s", s=4),
-                    in_=h_planes[:, g * PACK : (g + 1) * PACK, :].rearrange("p t (q s) -> p q t s", s=4),
-                )
+        def regroup(i):
+            h_planes = live["h_planes", i]
+            h_grouped = work.tile([P, PASSES, GROUP_COLS, PACK], BF16, name="h_grouped", align_bytes=64)
+            nc.vector.tensor_copy(
+                out=h_grouped[:, 0, :, :].rearrange("p (q s) t -> p q t s", s=4),
+                in_=h_planes[:, 0:PACK, :].rearrange("p t (q s) -> p q t s", s=4),
+            )
+            nc.scalar.copy(
+                out=h_grouped[:, 1, :, :].rearrange("p (q s) t -> p q t s", s=4),
+                in_=h_planes[:, PACK : 2 * PACK, :].rearrange("p t (q s) -> p q t s", s=4),
+            )
+            live["h_grouped", i] = h_grouped
+
+        def quantise(i):
+            h_grouped = live["h_grouped", i]
+            h_codes = work.tile([P, PASSES, GROUP_COLS], U32, name="h_codes", align_bytes=64)
+            h_scales = work.tile([P, PASSES, GROUP_COLS], U8, name="h_scales", align_bytes=64)
             for g in range(PASSES):
                 nc.vector.quantize_mx(
                     out=h_codes[:, g, :].bitcast(FP8X4),
                     scales=h_scales[:, g, :],
                     in_=h_grouped[:, g, :, :].rearrange("p r t -> p (r t)"),
                 )
+            live["h_codes", i] = h_codes
+            live["h_scales", i] = h_scales
 
-            fused = acc_psum.tile([P, TILES, W], F32)
+        def project(i):
+            h_codes = live["h_codes", i]
+            h_scales = live["h_scales", i]
+            fused = acc_psum.tile([P, TILES, W], F32, name="fused")
             for j in range(TILES):
                 tile_cols = slice(j * P, (j + 1) * P)
                 for g in range(PASSES):
@@ -154,14 +179,36 @@ def tile_latentattentionblock_pa_t_kernel(tc, x, ln_gamma, ln_beta, expand, out_
                         start=(g == 0),
                         stop=(g == PASSES - 1),
                     )
+            live["fused", i] = fused
 
-            results = out_pool.tile([P, 3, TILES, QK], F32)
+        def finish(i):
+            fused = live["fused", i]
+            results = out_pool.tile([P, 3, TILES, QK], F32, name="results")
             nc.scalar.copy(
                 out=results[:, 0:2, :, :],
                 in_=fused[:, :, 0 : 2 * QK].rearrange("p j (w c) -> p w j c", w=2),
             )
-            gelu = out_pool.tile([P, TILES, QK], F32)
+            gelu = out_pool.tile([P, TILES, QK], F32, name="gelu")
             nc.scalar.activation(out=gelu[:], in_=fused[:, :, 3 * QK : 4 * QK], func=ACT.Gelu)
-            nc.vector.tensor_tensor(out=results[:, 2, :, :], in0=fused[:, :, 2 * QK : 3 * QK], in1=gelu[:], op=ALU.mult)
+            nc.vector.tensor_tensor(
+                out=results[:, 2, :, :], in0=fused[:, :, 2 * QK : 3 * QK], in1=gelu[:], op=ALU.mult
+            )
             for w in range(3):
-                nc.sync.dma_start(out=out_rows[w][:, group_rows, :], in_=results[:, w, :, :])
+                nc.sync.dma_start(out=out_rows[w][:, i * TILES : (i + 1) * TILES, :], in_=results[:, w, :, :])
+
+        def run(stage, i):
+            if 0 <= i < GROUPS:
+                stage(i)
+
+        with tc.manual_schedule():
+            for i in range(X_BUFS - 1):
+                load(i)
+            for step in range(GROUPS + 4):
+                run(load, step + X_BUFS - 1)
+                run(statistics, step)
+                run(regroup, step - 2)
+                run(quantise, step - 2)
+                run(project, step - 3)
+                run(finish, step - 4)
+                run(normalise, step)
+                run(transpose_gain_shift, step - 1)

@@ -196,19 +196,12 @@ def tile_latentattentionblock_pa_t_kernel(tc, x, ln_gamma, ln_beta, expand, out_
             for w in range(3):
                 nc.sync.dma_start(out=out_rows[w][:, i * TILES : (i + 1) * TILES, :], in_=results[:, w, :, :])
 
-        def run(stage, i):
-            if 0 <= i < GROUPS:
-                stage(i)
-
-        with tc.manual_schedule():
-            for i in range(X_BUFS - 1):
-                load(i)
-            for step in range(GROUPS + 4):
-                run(load, step + X_BUFS - 1)
-                run(statistics, step)
-                run(regroup, step - 2)
-                run(quantise, step - 2)
-                run(project, step - 3)
-                run(finish, step - 4)
-                run(normalise, step)
-                run(transpose_gain_shift, step - 1)
+        for i in range(GROUPS):
+            load(i)
+            statistics(i)
+            normalise(i)
+            transpose_gain_shift(i)
+            regroup(i)
+            quantise(i)
+            project(i)
+            finish(i)

@@ -111,7 +111,8 @@ def tile_latentattentionblock_pa_t_kernel(tc, x, ln_gamma, ln_beta, expand, out_
             nc.gpsimd.tensor_tensor(out=rstd[:], in0=live["var_eps", i][:], in1=minus_half[:], op=ALU.pow)
             normed = work.tile([P, TILES, D], F32, name="normed")
             for j in range(TILES):
-                nc.gpsimd.tensor_scalar(
+                engine = nc.vector if j == TILES - 1 else nc.gpsimd
+                engine.tensor_scalar(
                     out=normed[:, j, :],
                     in0=x_sb[:, j, :],
                     scalar1=minus_mean[:, j : j + 1],

from contextlib import ExitStack

import concourse.mybir as mybir
from concourse.masks import make_identity

F32 = mybir.dt.float32
BF16 = mybir.dt.bfloat16
U32 = mybir.dt.uint32
U8 = mybir.dt.uint8
I32 = mybir.dt.int32
FP8X4 = mybir.dt.float8_e4m3fn_x4
ALU = mybir.AluOpType
ACT = mybir.ActivationFunctionType

P = 128
ROWS = 16 * 512
D = 1024
W = 128
QK = 32
EPS = 1e-5
PACK = 4
K_PASS = P * PACK
PASSES = D // K_PASS
CHUNKS = D // P
BN_MAX = 512
TILES = 4
GROUP_COLS = TILES * P
ROWS_PER_PARTITION = ROWS // P
GROUPS = ROWS_PER_PARTITION // TILES
X_BUFS = 4
STAGE_BUFS = 3

FLOPS = 2 * ROWS * D * W


def tile_latentattentionblock_pa_t_kernel(tc, x, ln_gamma, ln_beta, expand, out_0, out_1, out_2):
    nc = tc.nc
    x_rows = x.flatten_outer_dims().rearrange("(p j) d -> p j d", p=P)
    out_rows = [o.flatten_outer_dims().rearrange("(p j) c -> p j c", p=P) for o in (out_0, out_1, out_2)]

    with ExitStack() as stack:
        const = stack.enter_context(tc.tile_pool(name="const", bufs=1))

        ident_f32 = const.tile([P, P], F32)
        make_identity(nc, ident_f32[:])
        ident_bf16 = const.tile([P, P], BF16)
        make_identity(nc, ident_bf16[:])
        minus_half = const.tile([P, TILES], F32)
        nc.gpsimd.memset(minus_half[:], -0.5)

        vec_rows = const.tile([P, P], BF16)
        nc.vector.memset(vec_rows[:].bitcast(I32), 0)
        nc.scalar.dma_start(out=vec_rows[0:CHUNKS, :], in_=ln_gamma.rearrange("(c p) -> c p", p=P))
        nc.scalar.dma_start(out=vec_rows[CHUNKS : 2 * CHUNKS, :], in_=ln_beta.rearrange("(c p) -> c p", p=P))
        expand_sb = const.tile([W, D], BF16)
        nc.scalar.dma_start(out=expand_sb[:], in_=expand)

        gain_shift = const.tile([P, 2 * CHUNKS], F32)
        e_grouped = const.tile([P, PASSES, W, PACK], BF16, align_bytes=64)
        e_codes = const.tile([P, PASSES, W], U32, align_bytes=64)
        e_scales = const.tile([P, PASSES, W], U8, align_bytes=64)
        with tc.psum_pool(name="setup_psum", bufs=1) as setup_psum:
            vec_cols = setup_psum.tile([P, P], BF16)
            nc.tensor.transpose(vec_cols[:], vec_rows[:], ident_bf16[:])
            nc.vector.tensor_copy(out=gain_shift[:], in_=vec_cols[:, 0 : 2 * CHUNKS])
            for g in range(PASSES):
                e_t = setup_psum.tile([P, PACK, W], BF16, name="e_t%d" % g)
                for t in range(PACK):
                    c = PACK * g + t
                    nc.tensor.transpose(e_t[:, t, :], expand_sb[:, c * P : (c + 1) * P], ident_bf16[:])
                nc.vector.tensor_copy(out=e_grouped[:, g, :, :], in_=e_t[:].rearrange("p t o -> p o t"))
            nc.vector.quantize_mx(
                out=e_codes[:].rearrange("p g o -> p (g o)").bitcast(FP8X4),
                scales=e_scales[:].rearrange("p g o -> p (g o)"),
                in_=e_grouped[:].rearrange("p g o t -> p (g o t)"),
            )

        x_pool = stack.enter_context(tc.tile_pool(name="x_pool", bufs=X_BUFS))
        small = stack.enter_context(tc.tile_pool(name="small", bufs=STAGE_BUFS))
        work = stack.enter_context(tc.tile_pool(name="work", bufs=STAGE_BUFS))
        out_pool = stack.enter_context(tc.tile_pool(name="out_pool", bufs=STAGE_BUFS))
        xt_psum = stack.enter_context(tc.psum_pool(name="xt_psum", bufs=6))
        acc_psum = stack.enter_context(tc.psum_pool(name="acc_psum", bufs=2))

        live = {}

        def load(i):
            x_sb = x_pool.tile([P, TILES, D], BF16, name="x_sb")
            nc.sync.dma_start(out=x_sb[:], in_=x_rows[:, i * TILES : (i + 1) * TILES, :])
            live["x", i] = x_sb

        def statistics(i):
            x_sb = live["x", i]
            stats = small.tile([P, TILES, D // BN_MAX, 6], F32, name="stats")
            mean_var = small.tile([P, TILES, 2], F32, name="mean_var")
            for j in range(TILES):
                for b in range(D // BN_MAX):
                    nc.vector.bn_stats(out=stats[:, j, b, :], in_=x_sb[:, j, b * BN_MAX : (b + 1) * BN_MAX])
                nc.vector.bn_aggr(out=mean_var[:, j, :], in_=stats[:, j, :, :].rearrange("p b s -> p (b s)"))
            minus_mean = small.tile([P, TILES], F32, name="minus_mean")
            nc.vector.tensor_scalar_mul(out=minus_mean[:], in0=mean_var[:, :, 0], scalar1=-1.0)
            var_eps = small.tile([P, TILES], F32, name="var_eps")
            nc.vector.tensor_scalar_add(out=var_eps[:], in0=mean_var[:, :, 1], scalar1=EPS)
            live["minus_mean", i] = minus_mean
            live["var_eps", i] = var_eps

        def normalise(i):
            x_sb = live["x", i]
            minus_mean = live["minus_mean", i]
            rstd = small.tile([P, TILES], F32, name="rstd")
            nc.gpsimd.tensor_tensor(out=rstd[:], in0=live["var_eps", i][:], in1=minus_half[:], op=ALU.pow)
            normed = work.tile([P, TILES, D], F32, name="normed")
            for j in range(TILES):
                engine = nc.vector if j == TILES - 1 else nc.gpsimd
                engine.tensor_scalar(
                    out=normed[:, j, :],
                    in0=x_sb[:, j, :],
                    scalar1=minus_mean[:, j : j + 1],
                    scalar2=rstd[:, j : j + 1],
                    op0=ALU.add,
                    op1=ALU.mult,
                )
            live["normed", i] = normed

        def transpose_gain_shift(i):
            normed = live["normed", i]
            h_planes = work.tile([P, CHUNKS, GROUP_COLS], BF16, name="h_planes")
            for c in range(CHUNKS):
                normed_t = xt_psum.tile([P, TILES, P], F32, name="normed_t")
                for j in range(TILES):
                    nc.tensor.transpose(normed_t[:, j, :], normed[:, j, c * P : (c + 1) * P], ident_f32[:])
                nc.scalar.activation(
                    out=h_planes[:, c, :],
                    in_=normed_t[:].rearrange("p j r -> p (j r)"),
                    func=ACT.Identity,
                    scale=gain_shift[:, c : c + 1],
                    bias=gain_shift[:, CHUNKS + c : CHUNKS + c + 1],
                )
            live["h_planes", i] = h_planes

        def regroup(i):
            h_planes = live["h_planes", i]
            h_grouped = work.tile([P, PASSES, GROUP_COLS, PACK], BF16, name="h_grouped", align_bytes=64)
            nc.vector.tensor_copy(
                out=h_grouped[:, 0, :, :].rearrange("p (q s) t -> p q t s", s=4),
                in_=h_planes[:, 0:PACK, :].rearrange("p t (q s) -> p q t s", s=4),
            )
            nc.scalar.copy(
                out=h_grouped[:, 1, :, :].rearrange("p (q s) t -> p q t s", s=4),
                in_=h_planes[:, PACK : 2 * PACK, :].rearrange("p t (q s) -> p q t s", s=4),
            )
            live["h_grouped", i] = h_grouped

        def quantise(i):
            h_grouped = live["h_grouped", i]
            h_codes = work.tile([P, PASSES, GROUP_COLS], U32, name="h_codes", align_bytes=64)
            h_scales = work.tile([P, PASSES, GROUP_COLS], U8, name="h_scales", align_bytes=64)
            for g in range(PASSES):
                nc.vector.quantize_mx(
                    out=h_codes[:, g, :].bitcast(FP8X4),
                    scales=h_scales[:, g, :],
                    in_=h_grouped[:, g, :, :].rearrange("p r t -> p (r t)"),
                )
            live["h_codes", i] = h_codes
            live["h_scales", i] = h_scales

        def project(i):
            h_codes = live["h_codes", i]
            h_scales = live["h_scales", i]
            fused = acc_psum.tile([P, TILES, W], F32, name="fused")
            for j in range(TILES):
                tile_cols = slice(j * P, (j + 1) * P)
                for g in range(PASSES):
                    nc.tensor.matmul_mx(
                        out=fused[:, j, :],
                        lhsT=h_codes[:, g, tile_cols].bitcast(FP8X4),
                        lhsT_scale=h_scales[:, g, tile_cols],
                        rhs=e_codes[:, g, :].bitcast(FP8X4),
                        rhs_scale=e_scales[:, g, :],
                        start=(g == 0),
                        stop=(g == PASSES - 1),
                    )
            live["fused", i] = fused

        def finish(i):
            fused = live["fused", i]
            results = out_pool.tile([P, 3, TILES, QK], F32, name="results")
            nc.scalar.copy(
                out=results[:, 0:2, :, :],
                in_=fused[:, :, 0 : 2 * QK].rearrange("p j (w c) -> p w j c", w=2),
            )
            gelu = out_pool.tile([P, TILES, QK], F32, name="gelu")
            nc.scalar.activation(out=gelu[:], in_=fused[:, :, 3 * QK : 4 * QK], func=ACT.Gelu)
            nc.vector.tensor_tensor(
                out=results[:, 2, :, :], in0=fused[:, :, 2 * QK : 3 * QK], in1=gelu[:], op=ALU.mult
            )
            for w in range(3):
                nc.sync.dma_start(out=out_rows[w][:, i * TILES : (i + 1) * TILES, :], in_=results[:, w, :, :])

        for i in range(GROUPS):
            load(i)
            statistics(i)
            normalise(i)
            transpose_gain_shift(i)
            regroup(i)
            quantise(i)
            project(i)
            finish(i)
